import numpy as np
import ml_dtypes


def mxq(x, axis, fmt="e4m3"):
    dtype, down = {"e4m3": (ml_dtypes.float8_e4m3fn, 7), "e5m2": (ml_dtypes.float8_e5m2, 14)}[fmt]
    v = np.moveaxis(np.asarray(x, np.float32).astype(ml_dtypes.bfloat16).astype(np.float64), axis, -1)
    blocks = v.reshape(v.shape[:-1] + (-1, 32))
    amax = np.abs(blocks).max(-1, keepdims=True)
    byte = np.maximum(np.where(amax > 0, np.frexp(amax)[1] - 1 + 127, 0) - down, 1)
    scale = np.exp2(byte - 127.0)
    codes = (blocks / scale).astype(np.float32).astype(dtype).astype(np.float64)
    return np.moveaxis((codes * scale).reshape(v.shape), -1, axis)


WIDE = False


def mx_kscale(k):
    if not WIDE:
        return np.ones(k)
    levels = np.array([10, -10, 5, -5, 0])
    a = np.random.permutation(np.resize(levels, k // 512 * 4)).reshape(k // 512, 4)
    idx = np.arange(k)
    return np.exp2(a[idx // 512, idx % 128 // 32])


BF16 = ml_dtypes.bfloat16


def bf(x):
    return np.asarray(x, np.float32).astype(BF16)


def f64(x):
    return np.asarray(x).astype(np.float64)


E2M1 = np.array([0.0, 0.5, 1.0, 1.5, 2.0, 3.0, 4.0, 6.0, -0.0, -0.5, -1.0, -1.5, -2.0, -3.0, -4.0, -6.0])


def pack_weight(w, fmt):
    k, n = w.shape
    w = f64(bf(w)).reshape(k // 32, 32, n)
    amax = np.abs(w).max(1)
    if fmt == "e4m3":
        byte = np.frexp(amax)[1] - 1 + 127 - 7
    else:
        mant, ex = np.frexp(amax / 6.0)
        byte = np.where(mant > 0.5, ex, ex - 1) + 127
    byte = np.clip(np.where(amax > 0, byte, 1), 1, 254)
    scaled = (w * np.exp2(127.0 - byte)[:, None, :]).reshape(k, n).astype(np.float32)
    by_word = np.ascontiguousarray(scaled.reshape(k // 512, 128, 4, n).transpose(0, 1, 3, 2))
    if fmt == "e4m3":
        words = by_word.astype(ml_dtypes.float8_e4m3fn).view(np.uint8)
    else:
        c = by_word.astype(ml_dtypes.float4_e2m1fn).view(np.uint8) & 0xF
        words = c[..., 0::2] | (c[..., 1::2] << 4)
    return np.ascontiguousarray(words), np.ascontiguousarray(byte.astype(np.uint8).reshape(k // 512, 16, n))


def unpack_weight(words, scales, fmt):
    g, p, n, _ = words.shape
    if fmt == "e4m3":
        vals = np.ascontiguousarray(words).view(ml_dtypes.float8_e4m3fn).astype(np.float64)
    else:
        nib = np.empty((g, p, n, 4), np.uint8)
        nib[..., 0::2] = words & 0xF
        nib[..., 1::2] = words >> 4
        vals = E2M1[nib]
    vals = vals * np.repeat(np.exp2(scales.astype(np.float64) - 127.0), 8, axis=1)[..., None]
    return vals.transpose(0, 1, 3, 2).reshape(g * 512, n)


NS, NI, T = 1024, 512, 1025
NA = NS + NI
FMT = "e4m3"


def setup_inputs():
    s = mx_kscale(NA)
    r = s[:NS]
    A = np.random.standard_normal((NS, NS)) / np.sqrt(NA)
    B = np.random.standard_normal((NS, NI)) / np.sqrt(NA)
    x0 = np.random.standard_normal(NS) * 3.0
    V = np.random.standard_normal((T, NA))
    V[0, :NS] *= 3.0
    A_words, A_scales = pack_weight((A * r[:, None] / s[None, :NS]).T, FMT)
    B_words, B_scales = pack_weight((B * r[:, None] / s[None, NS:]).T, FMT)
    return {"A_words": A_words, "A_scales": A_scales, "B_words": B_words, "B_scales": B_scales, "x0": bf(x0 * r),
            "net_input": bf((V * s[None, :]).reshape(-1)), "T": T}


def reference(A_words, A_scales, B_words, B_scales, x0, net_input, T):
    At = unpack_weight(A_words, A_scales, FMT)
    Bt = unpack_weight(B_words, B_scales, FMT)
    ABt = np.concatenate([At, Bt], axis=0)
    n_all, n_state = ABt.shape
    V = f64(net_input).reshape(T, n_all)
    out0 = V[0, :n_state] - f64(x0)
    prop = mxq(V[:-1], 1, "e4m3") @ ABt
    out_rest = prop - V[1:, :n_state]
    return np.concatenate([out0, out_rest.reshape(-1)])

@@ -1,0 +1,148 @@
+from contextlib import ExitStack
+
+import concourse.mybir as mybir
+from concourse.masks import make_identity
+
+BF16 = mybir.dt.bfloat16
+F32 = mybir.dt.float32
+I32 = mybir.dt.int32
+U32 = mybir.dt.uint32
+U8 = mybir.dt.uint8
+FP8X4 = mybir.dt.float8_e4m3fn_x4
+
+P = 128
+PACK = 4
+K_PASS = P * PACK
+N_STATE = 1024
+N_ALL = 1536
+PASSES = N_ALL // K_PASS
+A_PASSES = N_STATE // K_PASS
+TILES = 8
+PAIRS = TILES // 2
+N_HALF = 512
+HALVES = N_STATE // N_HALF
+WORDS_PASS = K_PASS // 2
+QUADRANTS = 4
+ROW0_PARTS = 16
+
+FLOPS = 2 * P * TILES * N_ALL * N_STATE
+
+
+def tile_constrainnet_kernel(tc, A_words, A_scales, B_words, B_scales, x0, net_input, T, out):
+    nc = tc.nc
+    steps = T - 1
+    assert steps == P * TILES
+
+    v_now = net_input[0 : steps * N_ALL].rearrange("(p i k) -> p i k", i=TILES, k=N_ALL)
+    v_next = net_input[N_ALL : N_ALL + steps * N_ALL].rearrange("(p i k) -> p i k", i=TILES, k=N_ALL)
+    r_next = out[N_STATE : N_STATE + steps * N_STATE].rearrange("(p i n) -> p i n", i=TILES, n=N_STATE)
+
+    a_code_words = A_words.rearrange("g p n c -> g p (n c)").bitcast(I32)
+    b_code_words = B_words.rearrange("g p n c -> g p (n c)").bitcast(I32)
+    a_scale_words = A_scales.bitcast(I32)
+    b_scale_words = B_scales.bitcast(I32)
+
+    with ExitStack() as ctx:
+        ctx.enter_context(tc.manual_schedule())
+        keep = ctx.enter_context(tc.tile_pool(name="keep", bufs=1))
+        results = ctx.enter_context(tc.tile_pool(name="results", bufs=4))
+        flipped = ctx.enter_context(tc.psum_pool(name="flipped", bufs=4))
+        sums = ctx.enter_context(tc.psum_pool(name="sums", bufs=4))
+
+        v_sb = keep.tile([P, TILES, N_ALL], BF16)
+        last_next = keep.tile([P, N_STATE], BF16)
+        grouped = keep.tile([P, PASSES, TILES, P, PACK], BF16, align_bytes=64)
+        x_codes = keep.tile([P, PASSES, TILES, P], U32, align_bytes=64)
+        x_scales = keep.tile([P, PASSES, TILES, P], U8, align_bytes=64)
+        w_codes = keep.tile([P, PASSES, N_STATE], U32, align_bytes=64)
+        w_scales = keep.tile([P, PASSES, N_STATE], U8, align_bytes=64)
+        identity = keep.tile([P, P], F32)
+        first_state = keep.tile([ROW0_PARTS, N_STATE // ROW0_PARTS], BF16)
+        start_state = keep.tile([ROW0_PARTS, N_STATE // ROW0_PARTS], BF16)
+        row0 = keep.tile([ROW0_PARTS, N_STATE // ROW0_PARTS], F32)
+
+        v_words = v_sb[:].bitcast(F32)
+        grouped_words = grouped[:].bitcast(F32)
+        w_code_words = w_codes[:].bitcast(I32)
+        w_scale_words = w_scales[:].bitcast(I32)
+
+        nc.vector.memset(w_scale_words, 0)
+        make_identity(nc, identity[:])
+
+        def load_pair(j):
+            two = slice(2 * j, 2 * j + 2)
+            nc.sync.dma_start(out=v_sb[:, two, :], in_=v_now[:, two, :])
+
+        load_pair(0)
+        load_pair(1)
+        for quadrant in range(QUADRANTS):
+            rows = slice(4 * quadrant, 4 * quadrant + 4)
+            live = slice(32 * quadrant, 32 * quadrant + 4)
+            nc.sync.dma_start(
+                out=w_scale_words[live, 0:A_PASSES, :],
+                in_=a_scale_words[:, rows, :].rearrange("g r n -> r g n"),
+            )
+            nc.sync.dma_start(out=w_scale_words[live, A_PASSES, :], in_=b_scale_words[0, rows, :])
+        nc.sync.dma_start(out=first_state[:], in_=net_input[0:N_STATE].rearrange("(p c) -> p c", p=ROW0_PARTS))
+        nc.sync.dma_start(out=start_state[:], in_=x0.rearrange("(p c) -> p c", p=ROW0_PARTS))
+        load_pair(2)
+        load_pair(3)
+        for half in range(HALVES):
+            cols = slice(half * N_HALF, (half + 1) * N_HALF)
+            nc.sync.dma_start(
+                out=w_code_words[:, 0:A_PASSES, cols],
+                in_=a_code_words[:, :, cols].rearrange("g p n -> p g n"),
+            )
+            nc.sync.dma_start(out=w_code_words[:, A_PASSES, cols], in_=b_code_words[0, :, cols])
+        nc.sync.dma_start(out=last_next[:], in_=v_next[:, TILES - 1, 0:N_STATE])
+
+        def quantise_pair(j):
+            two = slice(2 * j, 2 * j + 2)
+            for g in range(PASSES):
+                nc.vector.quantize_mx(
+                    out=x_codes[:, g, two, :].rearrange("q i p -> q (i p)").bitcast(FP8X4),
+                    scales=x_scales[:, g, two, :].rearrange("q i p -> q (i p)"),
+                    in_=grouped[:, g, two, :, :].rearrange("q i p c -> q (i p c)"),
+                )
+
+        for j in range(PAIRS):
+            two = slice(2 * j, 2 * j + 2)
+            for g in range(PASSES):
+                turned = flipped.tile([P, 2, 2, P], F32)
+                for i in range(2):
+                    for u in range(2):
+                        nc.tensor.transpose(
+                            turned[:, i, u, :],
+                            v_words[:, 2 * j + i, g * WORDS_PASS + u : (g + 1) * WORDS_PASS : 2],
+                            identity[:],
+                        )
+                side_by_side = turned[:].rearrange("q i u p -> q i p u")
+                if g < A_PASSES:
+                    nc.scalar.copy(out=grouped_words[:, g, two, :, :], in_=side_by_side)
+                else:
+                    nc.vector.tensor_copy(out=grouped_words[:, g, two, :, :], in_=side_by_side)
+            if j > 0:
+                quantise_pair(j - 1)
+        quantise_pair(PAIRS - 1)
+
+        nc.vector.tensor_sub(out=row0[:], in0=first_state[:], in1=start_state[:])
+        nc.sync.dma_start(out=out[0:N_STATE].rearrange("(p c) -> p c", p=ROW0_PARTS), in_=row0[:])
+
+        for half in range(HALVES):
+            cols = slice(half * N_HALF, (half + 1) * N_HALF)
+            for i in range(TILES):
+                product = sums.tile([P, N_HALF], F32)
+                for g in range(PASSES):
+                    nc.tensor.matmul_mx(
+                        out=product[:],
+                        lhsT=x_codes[:, g, i, :].bitcast(FP8X4),
+                        lhsT_scale=x_scales[:, g, i, :],
+                        rhs=w_codes[:, g, cols].bitcast(FP8X4),
+                        rhs_scale=w_scales[:, g, cols],
+                        start=(g == 0),
+                        stop=(g == PASSES - 1),
+                    )
+                next_state = v_sb[:, i + 1, cols] if i + 1 < TILES else last_next[:, cols]
+                residual = results.tile([P, N_HALF], F32)
+                nc.vector.tensor_sub(out=residual[:], in0=product[:], in1=next_state)
+                nc.sync.dma_start(out=r_next[:, i, cols], in_=residual[:])

@@ -18,10 +18,12 @@ N_ALL = 1536
 PASSES = N_ALL // K_PASS
 A_PASSES = N_STATE // K_PASS
 TILES = 8
-PAIRS = TILES // 2
+SLABS = TILES * PASSES
+SLAB_WORDS = K_PASS // 2
+BANK_SLABS = 2
+BANKS = SLABS // BANK_SLABS
 N_HALF = 512
 HALVES = N_STATE // N_HALF
-WORDS_PASS = K_PASS // 2
 QUADRANTS = 4
 ROW0_PARTS = 16
 
@@ -51,9 +53,9 @@ def tile_constrainnet_kernel(tc, A_words, A_scales, B_words, B_scales, x0, net_i
 
         v_sb = keep.tile([P, TILES, N_ALL], BF16)
         last_next = keep.tile([P, N_STATE], BF16)
-        grouped = keep.tile([P, PASSES, TILES, P, PACK], BF16, align_bytes=64)
-        x_codes = keep.tile([P, PASSES, TILES, P], U32, align_bytes=64)
-        x_scales = keep.tile([P, PASSES, TILES, P], U8, align_bytes=64)
+        grouped = keep.tile([P, SLABS, P, PACK], BF16, align_bytes=64)
+        x_codes = keep.tile([P, SLABS, P], U32, align_bytes=64)
+        x_scales = keep.tile([P, SLABS, P], U8, align_bytes=64)
         w_codes = keep.tile([P, PASSES, N_STATE], U32, align_bytes=64)
         w_scales = keep.tile([P, PASSES, N_STATE], U8, align_bytes=64)
         identity = keep.tile([P, P], F32)
@@ -61,7 +63,7 @@ def tile_constrainnet_kernel(tc, A_words, A_scales, B_words, B_scales, x0, net_i
         start_state = keep.tile([ROW0_PARTS, N_STATE // ROW0_PARTS], BF16)
         row0 = keep.tile([ROW0_PARTS, N_STATE // ROW0_PARTS], F32)
 
-        v_words = v_sb[:].bitcast(F32)
+        v_words = v_sb[:].rearrange("p i k -> p (i k)").bitcast(F32)
         grouped_words = grouped[:].bitcast(F32)
         w_code_words = w_codes[:].bitcast(I32)
         w_scale_words = w_scales[:].bitcast(I32)
@@ -69,13 +71,12 @@ def tile_constrainnet_kernel(tc, A_words, A_scales, B_words, B_scales, x0, net_i
         nc.vector.memset(w_scale_words, 0)
         make_identity(nc, identity[:])
 
-        def load_pair(j):
-            two = slice(2 * j, 2 * j + 2)
-            nc.sync.dma_start(out=v_sb[:, two, :], in_=v_now[:, two, :])
+        nc.gpsimd.dma_start(out=first_state[:], in_=net_input[0:N_STATE].rearrange("(p c) -> p c", p=ROW0_PARTS))
+        nc.gpsimd.dma_start(out=start_state[:], in_=x0.rearrange("(p c) -> p c", p=ROW0_PARTS))
+        nc.gpsimd.tensor_sub(out=row0[:], in0=first_state[:], in1=start_state[:])
+        nc.gpsimd.dma_start(out=out[0:N_STATE].rearrange("(p c) -> p c", p=ROW0_PARTS), in_=row0[:])
 
-        load_pair(0)
-        load_pair(1)
-        for quadrant in range(QUADRANTS):
+        def load_scale_rows(quadrant):
             rows = slice(4 * quadrant, 4 * quadrant + 4)
             live = slice(32 * quadrant, 32 * quadrant + 4)
             nc.sync.dma_start(
@@ -83,10 +84,12 @@ def tile_constrainnet_kernel(tc, A_words, A_scales, B_words, B_scales, x0, net_i
                 in_=a_scale_words[:, rows, :].rearrange("g r n -> r g n"),
             )
             nc.sync.dma_start(out=w_scale_words[live, A_PASSES, :], in_=b_scale_words[0, rows, :])
-        nc.sync.dma_start(out=first_state[:], in_=net_input[0:N_STATE].rearrange("(p c) -> p c", p=ROW0_PARTS))
-        nc.sync.dma_start(out=start_state[:], in_=x0.rearrange("(p c) -> p c", p=ROW0_PARTS))
-        load_pair(2)
-        load_pair(3)
+
+        for turn in range(2):
+            for i in range(4 * turn, 4 * turn + 4):
+                nc.sync.dma_start(out=v_sb[:, i, :], in_=v_now[:, i, :])
+            for quadrant in range(2 * turn, 2 * turn + 2):
+                load_scale_rows(quadrant)
         for half in range(HALVES):
             cols = slice(half * N_HALF, (half + 1) * N_HALF)
             nc.sync.dma_start(
@@ -96,37 +99,36 @@ def tile_constrainnet_kernel(tc, A_words, A_scales, B_words, B_scales, x0, net_i
             nc.sync.dma_start(out=w_code_words[:, A_PASSES, cols], in_=b_code_words[0, :, cols])
         nc.sync.dma_start(out=last_next[:], in_=v_next[:, TILES - 1, 0:N_STATE])
 
-        def quantise_pair(j):
-            two = slice(2 * j, 2 * j + 2)
-            for g in range(PASSES):
-                nc.vector.quantize_mx(
-                    out=x_codes[:, g, two, :].rearrange("q i p -> q (i p)").bitcast(FP8X4),
-                    scales=x_scales[:, g, two, :].rearrange("q i p -> q (i p)"),
-                    in_=grouped[:, g, two, :, :].rearrange("q i p c -> q (i p c)"),
-                )
+        def slabs_of_bank(b):
+            return slice(b * BANK_SLABS, (b + 1) * BANK_SLABS)
 
-        for j in range(PAIRS):
-            two = slice(2 * j, 2 * j + 2)
-            for g in range(PASSES):
-                turned = flipped.tile([P, 2, 2, P], F32)
-                for i in range(2):
-                    for u in range(2):
-                        nc.tensor.transpose(
-                            turned[:, i, u, :],
-                            v_words[:, 2 * j + i, g * WORDS_PASS + u : (g + 1) * WORDS_PASS : 2],
-                            identity[:],
-                        )
-                side_by_side = turned[:].rearrange("q i u p -> q i p u")
-                if g < A_PASSES:
-                    nc.scalar.copy(out=grouped_words[:, g, two, :, :], in_=side_by_side)
-                else:
-                    nc.vector.tensor_copy(out=grouped_words[:, g, two, :, :], in_=side_by_side)
-            if j > 0:
-                quantise_pair(j - 1)
-        quantise_pair(PAIRS - 1)
+        def quantise_bank(b):
+            slabs = slabs_of_bank(b)
+            nc.vector.quantize_mx(
+                out=x_codes[:, slabs, :].rearrange("q s p -> q (s p)").bitcast(FP8X4),
+                scales=x_scales[:, slabs, :].rearrange("q s p -> q (s p)"),
+                in_=grouped[:, slabs, :, :].rearrange("q s p c -> q (s p c)"),
+            )
 
-        nc.vector.tensor_sub(out=row0[:], in0=first_state[:], in1=start_state[:])
-        nc.sync.dma_start(out=out[0:N_STATE].rearrange("(p c) -> p c", p=ROW0_PARTS), in_=row0[:])
+        for b in range(BANKS):
+            slabs = slabs_of_bank(b)
+            turned = flipped.tile([P, BANK_SLABS, 2, P], F32)
+            for s in range(BANK_SLABS):
+                first_word = (b * BANK_SLABS + s) * SLAB_WORDS
+                for u in range(2):
+                    nc.tensor.transpose(
+                        turned[:, s, u, :],
+                        v_words[:, first_word + u : first_word + SLAB_WORDS : 2],
+                        identity[:],
+                    )
+            side_by_side = turned[:].rearrange("q s u p -> q s p u")
+            if b % 3 == 2:
+                nc.vector.tensor_copy(out=grouped_words[:, slabs, :, :], in_=side_by_side)
+            else:
+                nc.scalar.copy(out=grouped_words[:, slabs, :, :], in_=side_by_side)
+            if b > 0:
+                quantise_bank(b - 1)
+        quantise_bank(BANKS - 1)
 
         for half in range(HALVES):
             cols = slice(half * N_HALF, (half + 1) * N_HALF)
@@ -135,8 +137,8 @@ def tile_constrainnet_kernel(tc, A_words, A_scales, B_words, B_scales, x0, net_i
                 for g in range(PASSES):
                     nc.tensor.matmul_mx(
                         out=product[:],
-                        lhsT=x_codes[:, g, i, :].bitcast(FP8X4),
-                        lhsT_scale=x_scales[:, g, i, :],
+                        lhsT=x_codes[:, PASSES * i + g, :].bitcast(FP8X4),
+                        lhsT_scale=x_scales[:, PASSES * i + g, :],
                         rhs=w_codes[:, g, cols].bitcast(FP8X4),
                         rhs_scale=w_scales[:, g, cols],
                         start=(g == 0),

@@ -25,6 +25,7 @@ BANKS = SLABS // BANK_SLABS
 N_HALF = 512
 HALVES = N_STATE // N_HALF
 QUADRANTS = 4
+LIVE_ROWS = 4
 ROW0_PARTS = 16
 
 FLOPS = 2 * P * TILES * N_ALL * N_STATE
@@ -57,7 +58,7 @@ def tile_constrainnet_kernel(tc, A_words, A_scales, B_words, B_scales, x0, net_i
         x_codes = keep.tile([P, SLABS, P], U32, align_bytes=64)
         x_scales = keep.tile([P, SLABS, P], U8, align_bytes=64)
         w_codes = keep.tile([P, PASSES, N_STATE], U32, align_bytes=64)
-        w_scales = keep.tile([P, PASSES, N_STATE], U8, align_bytes=64)
+        w_scales = keep.tile([P, N_STATE], U8, align_bytes=64)
         identity = keep.tile([P, P], F32)
         first_state = keep.tile([ROW0_PARTS, N_STATE // ROW0_PARTS], BF16)
         start_state = keep.tile([ROW0_PARTS, N_STATE // ROW0_PARTS], BF16)
@@ -77,13 +78,12 @@ def tile_constrainnet_kernel(tc, A_words, A_scales, B_words, B_scales, x0, net_i
         nc.gpsimd.dma_start(out=out[0:N_STATE].rearrange("(p c) -> p c", p=ROW0_PARTS), in_=row0[:])
 
         def load_scale_rows(quadrant):
-            rows = slice(4 * quadrant, 4 * quadrant + 4)
-            live = slice(32 * quadrant, 32 * quadrant + 4)
-            nc.sync.dma_start(
-                out=w_scale_words[live, 0:A_PASSES, :],
-                in_=a_scale_words[:, rows, :].rearrange("g r n -> r g n"),
-            )
-            nc.sync.dma_start(out=w_scale_words[live, A_PASSES, :], in_=b_scale_words[0, rows, :])
+            rows = slice(LIVE_ROWS * quadrant, LIVE_ROWS * (quadrant + 1))
+            first = 32 * quadrant
+            after_a = first + LIVE_ROWS * A_PASSES
+            after_b = first + LIVE_ROWS * PASSES
+            nc.sync.dma_start(out=w_scale_words[first:after_a, :], in_=a_scale_words[:, rows, :])
+            nc.sync.dma_start(out=w_scale_words[after_a:after_b, :], in_=b_scale_words[0, rows, :])
 
         for turn in range(2):
             for i in range(4 * turn, 4 * turn + 4):
@@ -140,7 +140,7 @@ def tile_constrainnet_kernel(tc, A_words, A_scales, B_words, B_scales, x0, net_i
                         lhsT=x_codes[:, PASSES * i + g, :].bitcast(FP8X4),
                         lhsT_scale=x_scales[:, PASSES * i + g, :],
                         rhs=w_codes[:, g, cols].bitcast(FP8X4),
-                        rhs_scale=w_scales[:, g, cols],
+                        rhs_scale=w_scales[LIVE_ROWS * g : P, cols],
                         start=(g == 0),
                         stop=(g == PASSES - 1),
                     )

@@ -48,9 +48,8 @@ def tile_constrainnet_kernel(tc, A_words, A_scales, B_words, B_scales, x0, net_i
     with ExitStack() as ctx:
         ctx.enter_context(tc.manual_schedule())
         keep = ctx.enter_context(tc.tile_pool(name="keep", bufs=1))
-        results = ctx.enter_context(tc.tile_pool(name="results", bufs=4))
-        flipped = ctx.enter_context(tc.psum_pool(name="flipped", bufs=4))
-        sums = ctx.enter_context(tc.psum_pool(name="sums", bufs=4))
+        results = ctx.enter_context(tc.tile_pool(name="results", bufs=8))
+        psum = ctx.enter_context(tc.psum_pool(name="psum", bufs=8))
 
         v_sb = keep.tile([P, TILES, N_ALL], BF16)
         last_next = keep.tile([P, N_STATE], BF16)
@@ -77,30 +76,63 @@ def tile_constrainnet_kernel(tc, A_words, A_scales, B_words, B_scales, x0, net_i
         nc.gpsimd.tensor_sub(out=row0[:], in0=first_state[:], in1=start_state[:])
         nc.gpsimd.dma_start(out=out[0:N_STATE].rearrange("(p c) -> p c", p=ROW0_PARTS), in_=row0[:])
 
-        def load_scale_rows(quadrant):
+        def load_v(i):
+            nc.sync.dma_start(out=v_sb[:, i, :], in_=v_now[:, i, :])
+
+        def load_a_scales(quadrant):
             rows = slice(LIVE_ROWS * quadrant, LIVE_ROWS * (quadrant + 1))
             first = 32 * quadrant
-            after_a = first + LIVE_ROWS * A_PASSES
-            after_b = first + LIVE_ROWS * PASSES
-            nc.sync.dma_start(out=w_scale_words[first:after_a, :], in_=a_scale_words[:, rows, :])
-            nc.sync.dma_start(out=w_scale_words[after_a:after_b, :], in_=b_scale_words[0, rows, :])
+            nc.sync.dma_start(out=w_scale_words[first : first + LIVE_ROWS * A_PASSES, :], in_=a_scale_words[:, rows, :])
 
-        for turn in range(2):
-            for i in range(4 * turn, 4 * turn + 4):
-                nc.sync.dma_start(out=v_sb[:, i, :], in_=v_now[:, i, :])
-            for quadrant in range(2 * turn, 2 * turn + 2):
-                load_scale_rows(quadrant)
-        for half in range(HALVES):
+        def load_b_scales(quadrant):
+            rows = slice(LIVE_ROWS * quadrant, LIVE_ROWS * (quadrant + 1))
+            first = 32 * quadrant + LIVE_ROWS * A_PASSES
+            nc.sync.dma_start(out=w_scale_words[first : first + LIVE_ROWS, :], in_=b_scale_words[0, rows, :])
+
+        def load_w(half, g):
             cols = slice(half * N_HALF, (half + 1) * N_HALF)
-            nc.sync.dma_start(
-                out=w_code_words[:, 0:A_PASSES, cols],
-                in_=a_code_words[:, :, cols].rearrange("g p n -> p g n"),
-            )
-            nc.sync.dma_start(out=w_code_words[:, A_PASSES, cols], in_=b_code_words[0, :, cols])
+            if g < A_PASSES:
+                nc.sync.dma_start(out=w_code_words[:, g, cols], in_=a_code_words[g, :, cols])
+            else:
+                nc.sync.dma_start(out=w_code_words[:, g, cols], in_=b_code_words[0, :, cols])
+
+        load_v(0)
+        for quadrant in range(QUADRANTS):
+            load_a_scales(quadrant)
+        load_v(1)
+        load_v(2)
+        load_v(3)
+        load_w(0, 0)
+        for quadrant in range(QUADRANTS):
+            load_b_scales(quadrant)
+        load_w(0, 1)
+        load_w(0, 2)
+        for g in range(PASSES):
+            load_w(1, g)
+        for i in range(4, TILES):
+            load_v(i)
         nc.sync.dma_start(out=last_next[:], in_=v_next[:, TILES - 1, 0:N_STATE])
 
         def slabs_of_bank(b):
             return slice(b * BANK_SLABS, (b + 1) * BANK_SLABS)
+
+        def transpose_bank(b, on_vector):
+            slabs = slabs_of_bank(b)
+            bank = psum.tile([P, N_HALF], F32)
+            turned = bank[:].rearrange("q (s u p) -> q s u p", s=BANK_SLABS, u=2)
+            for s in range(BANK_SLABS):
+                first_word = (b * BANK_SLABS + s) * SLAB_WORDS
+                for u in range(2):
+                    nc.tensor.transpose(
+                        turned[:, s, u, :],
+                        v_words[:, first_word + u : first_word + SLAB_WORDS : 2],
+                        identity[:],
+                    )
+            side_by_side = turned.rearrange("q s u p -> q s p u")
+            if on_vector:
+                nc.vector.tensor_copy(out=grouped_words[:, slabs, :, :], in_=side_by_side)
+            else:
+                nc.scalar.copy(out=grouped_words[:, slabs, :, :], in_=side_by_side)
 
         def quantise_bank(b):
             slabs = slabs_of_bank(b)
@@ -110,41 +142,63 @@ def tile_constrainnet_kernel(tc, A_words, A_scales, B_words, B_scales, x0, net_i
                 in_=grouped[:, slabs, :, :].rearrange("q s p c -> q (s p c)"),
             )
 
-        for b in range(BANKS):
-            slabs = slabs_of_bank(b)
-            turned = flipped.tile([P, BANK_SLABS, 2, P], F32)
-            for s in range(BANK_SLABS):
-                first_word = (b * BANK_SLABS + s) * SLAB_WORDS
-                for u in range(2):
-                    nc.tensor.transpose(
-                        turned[:, s, u, :],
-                        v_words[:, first_word + u : first_word + SLAB_WORDS : 2],
-                        identity[:],
-                    )
-            side_by_side = turned[:].rearrange("q s u p -> q s p u")
-            if b % 3 == 2:
-                nc.vector.tensor_copy(out=grouped_words[:, slabs, :, :], in_=side_by_side)
-            else:
-                nc.scalar.copy(out=grouped_words[:, slabs, :, :], in_=side_by_side)
+        def multiply(product, i, half, g):
+            cols = slice(half * N_HALF, (half + 1) * N_HALF)
+            nc.tensor.matmul_mx(
+                out=product[:],
+                lhsT=x_codes[:, PASSES * i + g, :].bitcast(FP8X4),
+                lhsT_scale=x_scales[:, PASSES * i + g, :],
+                rhs=w_codes[:, g, cols].bitcast(FP8X4),
+                rhs_scale=w_scales[LIVE_ROWS * g : P, cols],
+                start=(g == 0),
+                stop=(g == PASSES - 1),
+            )
+
+        def finish(product, i, half):
+            cols = slice(half * N_HALF, (half + 1) * N_HALF)
+            next_state = v_sb[:, i + 1, cols] if i + 1 < TILES else last_next[:, cols]
+            residual = results.tile([P, N_HALF], F32)
+            nc.vector.tensor_sub(out=residual[:], in0=product[:], in1=next_state)
+            nc.sync.dma_start(out=r_next[:, i, cols], in_=residual[:])
+
+        def whole_group(i, half):
+            bank = psum.tile([P, N_HALF], F32)
+            for g in range(PASSES):
+                multiply(bank, i, half, g)
+            finish(bank, i, half)
+
+        for b in range(6):
+            transpose_bank(b, b % 3 == 2)
             if b > 0:
                 quantise_bank(b - 1)
-        quantise_bank(BANKS - 1)
+        quantise_bank(5)
 
-        for half in range(HALVES):
-            cols = slice(half * N_HALF, (half + 1) * N_HALF)
-            for i in range(TILES):
-                product = sums.tile([P, N_HALF], F32)
-                for g in range(PASSES):
-                    nc.tensor.matmul_mx(
-                        out=product[:],
-                        lhsT=x_codes[:, PASSES * i + g, :].bitcast(FP8X4),
-                        lhsT_scale=x_scales[:, PASSES * i + g, :],
-                        rhs=w_codes[:, g, cols].bitcast(FP8X4),
-                        rhs_scale=w_scales[LIVE_ROWS * g : P, cols],
-                        start=(g == 0),
-                        stop=(g == PASSES - 1),
-                    )
-                next_state = v_sb[:, i + 1, cols] if i + 1 < TILES else last_next[:, cols]
-                residual = results.tile([P, N_HALF], F32)
-                nc.vector.tensor_sub(out=residual[:], in0=product[:], in1=next_state)
-                nc.sync.dma_start(out=r_next[:, i, cols], in_=residual[:])
+        open_groups = []
+        for i in range(4):
+            bank = psum.tile([P, N_HALF], F32)
+            open_groups.append(bank)
+        for g in range(PASSES):
+            for i in range(4):
+                multiply(open_groups[i], i, 0, g)
+        for i in range(4):
+            finish(open_groups[i], i, 0)
+
+        whole_group(0, 1)
+        whole_group(1, 1)
+        for b in range(6, 9):
+            transpose_bank(b, False)
+        for b in range(6, 9):
+            quantise_bank(b)
+        whole_group(2, 1)
+        whole_group(3, 1)
+        whole_group(4, 0)
+        whole_group(4, 1)
+        for b in range(9, 12):
+            transpose_bank(b, False)
+        for b in range(9, 12):
+            quantise_bank(b)
+        whole_group(5, 0)
+        whole_group(5, 1)
+        for i in range(6, TILES):
+            for half in range(HALVES):
+                whole_group(i, half)

@@ -53,6 +53,7 @@ def tile_constrainnet_kernel(tc, A_words, A_scales, B_words, B_scales, x0, net_i
 
         v_sb = keep.tile([P, TILES, N_ALL], BF16)
         last_next = keep.tile([P, N_STATE], BF16)
+        sorted_words = keep.tile([P, SLABS // 2, 2, P], F32)
         grouped = keep.tile([P, SLABS, P, PACK], BF16, align_bytes=64)
         x_codes = keep.tile([P, SLABS, P], U32, align_bytes=64)
         x_scales = keep.tile([P, SLABS, P], U8, align_bytes=64)
@@ -107,10 +108,12 @@ def tile_constrainnet_kernel(tc, A_words, A_scales, B_words, B_scales, x0, net_i
             load_b_scales(quadrant)
         load_w(0, 1)
         load_w(0, 2)
+        load_v(4)
+        load_v(5)
         for g in range(PASSES):
             load_w(1, g)
-        for i in range(4, TILES):
-            load_v(i)
+        load_v(6)
+        load_v(7)
         nc.sync.dma_start(out=last_next[:], in_=v_next[:, TILES - 1, 0:N_STATE])
 
         def slabs_of_bank(b):
@@ -121,18 +124,28 @@ def tile_constrainnet_kernel(tc, A_words, A_scales, B_words, B_scales, x0, net_i
             bank = psum.tile([P, N_HALF], F32)
             turned = bank[:].rearrange("q (s u p) -> q s u p", s=BANK_SLABS, u=2)
             for s in range(BANK_SLABS):
-                first_word = (b * BANK_SLABS + s) * SLAB_WORDS
+                slab = b * BANK_SLABS + s
+                first_word = slab * SLAB_WORDS
                 for u in range(2):
-                    nc.tensor.transpose(
-                        turned[:, s, u, :],
-                        v_words[:, first_word + u : first_word + SLAB_WORDS : 2],
-                        identity[:],
-                    )
+                    if slab < SLABS // 2:
+                        source = v_words[:, first_word + u : first_word + SLAB_WORDS : 2]
+                    else:
+                        source = sorted_words[:, slab - SLABS // 2, u, :]
+                    nc.tensor.transpose(turned[:, s, u, :], source, identity[:])
             side_by_side = turned.rearrange("q s u p -> q s p u")
             if on_vector:
                 nc.vector.tensor_copy(out=grouped_words[:, slabs, :, :], in_=side_by_side)
             else:
                 nc.scalar.copy(out=grouped_words[:, slabs, :, :], in_=side_by_side)
+
+        def sort_words(i):
+            first_slab = PASSES * i - SLABS // 2
+            nc.scalar.copy(
+                out=sorted_words[:, first_slab : first_slab + PASSES, :, :],
+                in_=v_words[:, PASSES * i * SLAB_WORDS : PASSES * (i + 1) * SLAB_WORDS].rearrange(
+                    "p (s q u) -> p s u q", s=PASSES, u=2
+                ),
+            )
 
         def quantise_bank(b):
             slabs = slabs_of_bank(b)
@@ -183,21 +196,39 @@ def tile_constrainnet_kernel(tc, A_words, A_scales, B_words, B_scales, x0, net_i
         for i in range(4):
             finish(open_groups[i], i, 0)
 
-        whole_group(0, 1)
-        whole_group(1, 1)
+        sort_words(4)
+        sort_words(5)
+
+        open_groups = []
+        for i in range(4):
+            bank = psum.tile([P, N_HALF], F32)
+            open_groups.append(bank)
+        for i in range(4):
+            multiply(open_groups[i], i, 1, 0)
         for b in range(6, 9):
             transpose_bank(b, False)
+        sort_words(6)
+        sort_words(7)
+        for i in range(4):
+            multiply(open_groups[i], i, 1, 1)
         for b in range(6, 9):
             quantise_bank(b)
-        whole_group(2, 1)
-        whole_group(3, 1)
+        for i in range(4):
+            multiply(open_groups[i], i, 1, 2)
+        for i in range(4):
+            finish(open_groups[i], i, 1)
+
         whole_group(4, 0)
         whole_group(4, 1)
         for b in range(9, 12):
             transpose_bank(b, False)
-        for b in range(9, 12):
-            quantise_bank(b)
-        whole_group(5, 0)
+        bank5 = psum.tile([P, N_HALF], F32, tag="bank")
+        for g in range(PASSES):
+            multiply(bank5, 5, 0, g)
+        quantise_bank(9)
+        quantise_bank(10)
+        finish(bank5, 5, 0)
+        quantise_bank(11)
         whole_group(5, 1)
         for i in range(6, TILES):
             for half in range(HALVES):

@@ -24,6 +24,7 @@ BANK_SLABS = 2
 BANKS = SLABS // BANK_SLABS
 N_HALF = 512
 HALVES = N_STATE // N_HALF
+N_QUARTER = 256
 QUADRANTS = 4
 LIVE_ROWS = 4
 ROW0_PARTS = 16
@@ -59,6 +60,7 @@ def tile_constrainnet_kernel(tc, A_words, A_scales, B_words, B_scales, x0, net_i
         x_scales = keep.tile([P, SLABS, P], U8, align_bytes=64)
         w_codes = keep.tile([P, PASSES, N_STATE], U32, align_bytes=64)
         w_scales = keep.tile([P, N_STATE], U8, align_bytes=64)
+        b_plane = keep.tile([P, N_STATE], U8, align_bytes=64)
         identity = keep.tile([P, P], F32)
         first_state = keep.tile([ROW0_PARTS, N_STATE // ROW0_PARTS], BF16)
         start_state = keep.tile([ROW0_PARTS, N_STATE // ROW0_PARTS], BF16)
@@ -68,8 +70,10 @@ def tile_constrainnet_kernel(tc, A_words, A_scales, B_words, B_scales, x0, net_i
         grouped_words = grouped[:].bitcast(F32)
         w_code_words = w_codes[:].bitcast(I32)
         w_scale_words = w_scales[:].bitcast(I32)
+        b_plane_words = b_plane[:].bitcast(I32)
 
         nc.vector.memset(w_scale_words, 0)
+        nc.vector.memset(b_plane_words, 0)
         make_identity(nc, identity[:])
 
         nc.gpsimd.dma_start(out=first_state[:], in_=net_input[0:N_STATE].rearrange("(p c) -> p c", p=ROW0_PARTS))
@@ -87,8 +91,8 @@ def tile_constrainnet_kernel(tc, A_words, A_scales, B_words, B_scales, x0, net_i
 
         def load_b_scales(quadrant):
             rows = slice(LIVE_ROWS * quadrant, LIVE_ROWS * (quadrant + 1))
-            first = 32 * quadrant + LIVE_ROWS * A_PASSES
-            nc.sync.dma_start(out=w_scale_words[first : first + LIVE_ROWS, :], in_=b_scale_words[0, rows, :])
+            first = 32 * quadrant
+            nc.sync.dma_start(out=b_plane_words[first : first + LIVE_ROWS, :], in_=b_scale_words[0, rows, :])
 
         def load_w(half, g):
             cols = slice(half * N_HALF, (half + 1) * N_HALF)
@@ -155,30 +159,30 @@ def tile_constrainnet_kernel(tc, A_words, A_scales, B_words, B_scales, x0, net_i
                 in_=grouped[:, slabs, :, :].rearrange("q s p c -> q (s p c)"),
             )
 
-        def multiply(product, i, half, g):
-            cols = slice(half * N_HALF, (half + 1) * N_HALF)
+        def multiply(product, i, half, g, width=N_HALF, skip=0):
+            cols = slice(half * N_HALF + skip, half * N_HALF + skip + width)
             nc.tensor.matmul_mx(
-                out=product[:],
+                out=product[:, 0:width],
                 lhsT=x_codes[:, PASSES * i + g, :].bitcast(FP8X4),
                 lhsT_scale=x_scales[:, PASSES * i + g, :],
                 rhs=w_codes[:, g, cols].bitcast(FP8X4),
-                rhs_scale=w_scales[LIVE_ROWS * g : P, cols],
+                rhs_scale=(w_scales[LIVE_ROWS * g : P, cols] if g < A_PASSES else b_plane[:, cols]),
                 start=(g == 0),
                 stop=(g == PASSES - 1),
             )
 
-        def finish(product, i, half):
-            cols = slice(half * N_HALF, (half + 1) * N_HALF)
+        def finish(product, i, half, width=N_HALF, skip=0):
+            cols = slice(half * N_HALF + skip, half * N_HALF + skip + width)
             next_state = v_sb[:, i + 1, cols] if i + 1 < TILES else last_next[:, cols]
             residual = results.tile([P, N_HALF], F32)
-            nc.vector.tensor_sub(out=residual[:], in0=product[:], in1=next_state)
-            nc.sync.dma_start(out=r_next[:, i, cols], in_=residual[:])
+            nc.vector.tensor_sub(out=residual[:, 0:width], in0=product[:, 0:width], in1=next_state)
+            nc.sync.dma_start(out=r_next[:, i, cols], in_=residual[:, 0:width])
 
-        def whole_group(i, half):
+        def whole_group(i, half, width=N_HALF, skip=0):
             bank = psum.tile([P, N_HALF], F32)
             for g in range(PASSES):
-                multiply(bank, i, half, g)
-            finish(bank, i, half)
+                multiply(bank, i, half, g, width, skip)
+            finish(bank, i, half, width, skip)
 
         for b in range(6):
             transpose_bank(b, b % 3 == 2)
@@ -230,6 +234,8 @@ def tile_constrainnet_kernel(tc, A_words, A_scales, B_words, B_scales, x0, net_i
         finish(bank5, 5, 0)
         quantise_bank(11)
         whole_group(5, 1)
-        for i in range(6, TILES):
-            for half in range(HALVES):
-                whole_group(i, half)
+        whole_group(6, 0)
+        whole_group(6, 1)
+        whole_group(7, 0)
+        whole_group(7, 1, N_QUARTER, 0)
+        whole_group(7, 1, N_QUARTER, N_QUARTER)

@@ -185,7 +185,7 @@ def tile_constrainnet_kernel(tc, A_words, A_scales, B_words, B_scales, x0, net_i
             finish(bank, i, half, width, skip)
 
         for b in range(6):
-            transpose_bank(b, b % 3 == 2)
+            transpose_bank(b, False)
             if b > 0:
                 quantise_bank(b - 1)
         quantise_bank(5)

@@ -101,21 +101,19 @@ def tile_constrainnet_kernel(tc, A_words, A_scales, B_words, B_scales, x0, net_i
             else:
                 nc.sync.dma_start(out=w_code_words[:, g, cols], in_=b_code_words[0, :, cols])
 
-        load_v(0)
+        for i in range(4):
+            load_v(i)
         for quadrant in range(QUADRANTS):
             load_a_scales(quadrant)
-        load_v(1)
-        load_v(2)
-        load_v(3)
-        load_w(0, 0)
+        for g in range(PASSES):
+            load_w(0, g)
         for quadrant in range(QUADRANTS):
             load_b_scales(quadrant)
-        load_w(0, 1)
-        load_w(0, 2)
         load_v(4)
+        load_w(1, 0)
         load_v(5)
-        for g in range(PASSES):
-            load_w(1, g)
+        load_w(1, 1)
+        load_w(1, 2)
         load_v(6)
         load_v(7)
         nc.sync.dma_start(out=last_next[:], in_=v_next[:, TILES - 1, 0:N_STATE])

@@ -65,6 +65,7 @@ def tile_constrainnet_kernel(tc, A_words, A_scales, B_words, B_scales, x0, net_i
         first_state = keep.tile([ROW0_PARTS, N_STATE // ROW0_PARTS], BF16)
         start_state = keep.tile([ROW0_PARTS, N_STATE // ROW0_PARTS], BF16)
         row0 = keep.tile([ROW0_PARTS, N_STATE // ROW0_PARTS], F32)
+        idle_values = keep.tile([P, N_HALF], BF16)
 
         v_words = v_sb[:].rearrange("p i k -> p (i k)").bitcast(F32)
         grouped_words = grouped[:].bitcast(F32)
@@ -72,6 +73,7 @@ def tile_constrainnet_kernel(tc, A_words, A_scales, B_words, B_scales, x0, net_i
         w_scale_words = w_scales[:].bitcast(I32)
         b_plane_words = b_plane[:].bitcast(I32)
 
+        nc.vector.memset(idle_values[:], 0.0)
         nc.vector.memset(w_scale_words, 0)
         nc.vector.memset(b_plane_words, 0)
         make_identity(nc, identity[:])
@@ -182,10 +184,21 @@ def tile_constrainnet_kernel(tc, A_words, A_scales, B_words, B_scales, x0, net_i
                 multiply(bank, i, half, g, width, skip)
             finish(bank, i, half, width, skip)
 
+        bank = psum.tile([P, N_HALF], F32)
+        idle_bank = bank
+
+        def idle_matmul():
+            nc.tensor.matmul(idle_bank[:], lhsT=idle_values[:, 0:P], rhs=idle_values[:], start=True, stop=True)
+
+        for n in range(4):
+            idle_matmul()
+
         for b in range(6):
             transpose_bank(b, False)
             if b > 0:
                 quantise_bank(b - 1)
+            if b in (1, 3):
+                idle_matmul()
         quantise_bank(5)
 
         open_groups = []

from contextlib import ExitStack

import concourse.mybir as mybir
from concourse.masks import make_identity

BF16 = mybir.dt.bfloat16
F32 = mybir.dt.float32
I32 = mybir.dt.int32
U32 = mybir.dt.uint32
U8 = mybir.dt.uint8
FP8X4 = mybir.dt.float8_e4m3fn_x4

P = 128
PACK = 4
K_PASS = P * PACK
N_STATE = 1024
N_ALL = 1536
PASSES = N_ALL // K_PASS
A_PASSES = N_STATE // K_PASS
TILES = 8
SLABS = TILES * PASSES
SLAB_WORDS = K_PASS // 2
BANK_SLABS = 2
BANKS = SLABS // BANK_SLABS
N_HALF = 512
HALVES = N_STATE // N_HALF
N_QUARTER = 256
QUADRANTS = 4
LIVE_ROWS = 4
ROW0_PARTS = 16

FLOPS = 2 * P * TILES * N_ALL * N_STATE


def tile_constrainnet_kernel(tc, A_words, A_scales, B_words, B_scales, x0, net_input, T, out):
    nc = tc.nc
    steps = T - 1
    assert steps == P * TILES

    v_now = net_input[0 : steps * N_ALL].rearrange("(p i k) -> p i k", i=TILES, k=N_ALL)
    v_next = net_input[N_ALL : N_ALL + steps * N_ALL].rearrange("(p i k) -> p i k", i=TILES, k=N_ALL)
    r_next = out[N_STATE : N_STATE + steps * N_STATE].rearrange("(p i n) -> p i n", i=TILES, n=N_STATE)

    a_code_words = A_words.rearrange("g p n c -> g p (n c)").bitcast(I32)
    b_code_words = B_words.rearrange("g p n c -> g p (n c)").bitcast(I32)
    a_scale_words = A_scales.bitcast(I32)
    b_scale_words = B_scales.bitcast(I32)

    with ExitStack() as ctx:
        ctx.enter_context(tc.manual_schedule())
        keep = ctx.enter_context(tc.tile_pool(name="keep", bufs=1))
        results = ctx.enter_context(tc.tile_pool(name="results", bufs=8))
        psum = ctx.enter_context(tc.psum_pool(name="psum", bufs=8))

        v_sb = keep.tile([P, TILES, N_ALL], BF16)
        last_next = keep.tile([P, N_STATE], BF16)
        sorted_words = keep.tile([P, SLABS // 2, 2, P], F32)
        grouped = keep.tile([P, SLABS, P, PACK], BF16, align_bytes=64)
        x_codes = keep.tile([P, SLABS, P], U32, align_bytes=64)
        x_scales = keep.tile([P, SLABS, P], U8, align_bytes=64)
        w_codes = keep.tile([P, PASSES, N_STATE], U32, align_bytes=64)
        w_scales = keep.tile([P, N_STATE], U8, align_bytes=64)
        b_plane = keep.tile([P, N_STATE], U8, align_bytes=64)
        identity = keep.tile([P, P], F32)
        first_state = keep.tile([ROW0_PARTS, N_STATE // ROW0_PARTS], BF16)
        start_state = keep.tile([ROW0_PARTS, N_STATE // ROW0_PARTS], BF16)
        row0 = keep.tile([ROW0_PARTS, N_STATE // ROW0_PARTS], F32)
        idle_values = keep.tile([P, N_HALF], BF16)

        v_words = v_sb[:].rearrange("p i k -> p (i k)").bitcast(F32)
        grouped_words = grouped[:].bitcast(F32)
        w_code_words = w_codes[:].bitcast(I32)
        w_scale_words = w_scales[:].bitcast(I32)
        b_plane_words = b_plane[:].bitcast(I32)

        nc.vector.memset(idle_values[:], 0.0)
        nc.vector.memset(w_scale_words, 0)
        nc.vector.memset(b_plane_words, 0)
        make_identity(nc, identity[:])

        nc.gpsimd.dma_start(out=first_state[:], in_=net_input[0:N_STATE].rearrange("(p c) -> p c", p=ROW0_PARTS))
        nc.gpsimd.dma_start(out=start_state[:], in_=x0.rearrange("(p c) -> p c", p=ROW0_PARTS))
        nc.gpsimd.tensor_sub(out=row0[:], in0=first_state[:], in1=start_state[:])
        nc.gpsimd.dma_start(out=out[0:N_STATE].rearrange("(p c) -> p c", p=ROW0_PARTS), in_=row0[:])

        def load_v(i):
            nc.sync.dma_start(out=v_sb[:, i, :], in_=v_now[:, i, :])

        def load_a_scales(quadrant):
            rows = slice(LIVE_ROWS * quadrant, LIVE_ROWS * (quadrant + 1))
            first = 32 * quadrant
            nc.sync.dma_start(out=w_scale_words[first : first + LIVE_ROWS * A_PASSES, :], in_=a_scale_words[:, rows, :])

        def load_b_scales(quadrant):
            rows = slice(LIVE_ROWS * quadrant, LIVE_ROWS * (quadrant + 1))
            first = 32 * quadrant
            nc.sync.dma_start(out=b_plane_words[first : first + LIVE_ROWS, :], in_=b_scale_words[0, rows, :])

        def load_w(half, g):
            cols = slice(half * N_HALF, (half + 1) * N_HALF)
            if g < A_PASSES:
                nc.sync.dma_start(out=w_code_words[:, g, cols], in_=a_code_words[g, :, cols])
            else:
                nc.sync.dma_start(out=w_code_words[:, g, cols], in_=b_code_words[0, :, cols])

        for i in range(4):
            load_v(i)
        for quadrant in range(QUADRANTS):
            load_a_scales(quadrant)
        for g in range(PASSES):
            load_w(0, g)
        for quadrant in range(QUADRANTS):
            load_b_scales(quadrant)
        load_v(4)
        load_w(1, 0)
        load_v(5)
        load_w(1, 1)
        load_w(1, 2)
        load_v(6)
        load_v(7)
        nc.sync.dma_start(out=last_next[:], in_=v_next[:, TILES - 1, 0:N_STATE])

        def slabs_of_bank(b):
            return slice(b * BANK_SLABS, (b + 1) * BANK_SLABS)

        def transpose_bank(b, on_vector):
            slabs = slabs_of_bank(b)
            bank = psum.tile([P, N_HALF], F32)
            turned = bank[:].rearrange("q (s u p) -> q s u p", s=BANK_SLABS, u=2)
            for s in range(BANK_SLABS):
                slab = b * BANK_SLABS + s
                first_word = slab * SLAB_WORDS
                for u in range(2):
                    if slab < SLABS // 2:
                        source = v_words[:, first_word + u : first_word + SLAB_WORDS : 2]
                    else:
                        source = sorted_words[:, slab - SLABS // 2, u, :]
                    nc.tensor.transpose(turned[:, s, u, :], source, identity[:])
            side_by_side = turned.rearrange("q s u p -> q s p u")
            if on_vector:
                nc.vector.tensor_copy(out=grouped_words[:, slabs, :, :], in_=side_by_side)
            else:
                nc.scalar.copy(out=grouped_words[:, slabs, :, :], in_=side_by_side)

        def sort_words(i):
            first_slab = PASSES * i - SLABS // 2
            nc.scalar.copy(
                out=sorted_words[:, first_slab : first_slab + PASSES, :, :],
                in_=v_words[:, PASSES * i * SLAB_WORDS : PASSES * (i + 1) * SLAB_WORDS].rearrange(
                    "p (s q u) -> p s u q", s=PASSES, u=2
                ),
            )

        def quantise_bank(b):
            slabs = slabs_of_bank(b)
            nc.vector.quantize_mx(
                out=x_codes[:, slabs, :].rearrange("q s p -> q (s p)").bitcast(FP8X4),
                scales=x_scales[:, slabs, :].rearrange("q s p -> q (s p)"),
                in_=grouped[:, slabs, :, :].rearrange("q s p c -> q (s p c)"),
            )

        def multiply(product, i, half, g, width=N_HALF, skip=0):
            cols = slice(half * N_HALF + skip, half * N_HALF + skip + width)
            nc.tensor.matmul_mx(
                out=product[:, 0:width],
                lhsT=x_codes[:, PASSES * i + g, :].bitcast(FP8X4),
                lhsT_scale=x_scales[:, PASSES * i + g, :],
                rhs=w_codes[:, g, cols].bitcast(FP8X4),
                rhs_scale=(w_scales[LIVE_ROWS * g : P, cols] if g < A_PASSES else b_plane[:, cols]),
                start=(g == 0),
                stop=(g == PASSES - 1),
            )

        def finish(product, i, half, width=N_HALF, skip=0):
            cols = slice(half * N_HALF + skip, half * N_HALF + skip + width)
            next_state = v_sb[:, i + 1, cols] if i + 1 < TILES else last_next[:, cols]
            residual = results.tile([P, N_HALF], F32)
            nc.vector.tensor_sub(out=residual[:, 0:width], in0=product[:, 0:width], in1=next_state)
            nc.sync.dma_start(out=r_next[:, i, cols], in_=residual[:, 0:width])

        def whole_group(i, half, width=N_HALF, skip=0):
            bank = psum.tile([P, N_HALF], F32)
            for g in range(PASSES):
                multiply(bank, i, half, g, width, skip)
            finish(bank, i, half, width, skip)

        bank = psum.tile([P, N_HALF], F32)
        idle_bank = bank

        def idle_matmul():
            nc.tensor.matmul(idle_bank[:], lhsT=idle_values[:, 0:P], rhs=idle_values[:], start=True, stop=True)

        for n in range(4):
            idle_matmul()

        for b in range(6):
            transpose_bank(b, False)
            if b > 0:
                quantise_bank(b - 1)
            if b in (1, 3):
                idle_matmul()
        quantise_bank(5)

        open_groups = []
        for i in range(4):
            bank = psum.tile([P, N_HALF], F32)
            open_groups.append(bank)
        for g in range(PASSES):
            for i in range(4):
                multiply(open_groups[i], i, 0, g)
        for i in range(4):
            finish(open_groups[i], i, 0)

        sort_words(4)
        sort_words(5)

        open_groups = []
        for i in range(4):
            bank = psum.tile([P, N_HALF], F32)
            open_groups.append(bank)
        for i in range(4):
            multiply(open_groups[i], i, 1, 0)
        for b in range(6, 9):
            transpose_bank(b, False)
        sort_words(6)
        sort_words(7)
        for i in range(4):
            multiply(open_groups[i], i, 1, 1)
        for b in range(6, 9):
            quantise_bank(b)
        for i in range(4):
            multiply(open_groups[i], i, 1, 2)
        for i in range(4):
            finish(open_groups[i], i, 1)

        whole_group(4, 0)
        whole_group(4, 1)
        for b in range(9, 12):
            transpose_bank(b, False)
        bank5 = psum.tile([P, N_HALF], F32, tag="bank")
        for g in range(PASSES):
            multiply(bank5, 5, 0, g)
        quantise_bank(9)
        quantise_bank(10)
        finish(bank5, 5, 0)
        quantise_bank(11)
        whole_group(5, 1)
        whole_group(6, 0)
        whole_group(6, 1)
        whole_group(7, 0)
        whole_group(7, 1, N_QUARTER, 0)
        whole_group(7, 1, N_QUARTER, N_QUARTER)
